import numpy as np
import ml_dtypes

BF16 = ml_dtypes.bfloat16


def bf(x):
    return np.asarray(x, np.float32).astype(BF16)


def f32(x):
    return np.asarray(x, np.float32)


def f64(x):
    return np.asarray(x).astype(np.float64)


def striped(idx):
    return np.tile(idx.reshape(-1, 16).T, (8, 1))


S, D, B, N = 2048, 128, 512, 1024
BW_NOISE = 0.05


def relu(v):
    return np.maximum(v, 0.0)


def setup_inputs():
    sn = np.random.standard_normal
    return {
        "table": bf(sn((S, D))),
        "w1": bf(sn((D, D)) / np.sqrt(D)),
        "b1": f32(0.1 * sn((D, 1))),
        "w2": bf(sn((D, D)) * np.sqrt(2.0 / D)),
        "b2": f32(0.1 * sn((D, 1))),
        "w3": bf(sn((D, D)) * np.sqrt(2.0 / D)),
        "b3": f32(0.1 * sn((D, 1))),
        "bw": f32(BW_NOISE * sn((D, D, D)) + np.eye(D)[:, None, :]),
        "bd": f32((1.0 + 0.1 * sn((D, D))) / np.sqrt(D)),
        "boff": f32(0.1 * sn((D, 1))),
        "wc1": bf(sn((D, D)) / np.sqrt(D)),
        "bc1": f32(0.1 * sn((D, 1))),
        "offs": striped(np.random.permutation(np.tile(np.arange(S), 2))[:N]),
    }


def reference(table, w1, b1, w2, b2, w3, b3, bw, bd, boff, wc1, bc1, offs):
    idx = offs[:16].T.reshape(-1)
    h = relu(f64(w1).T @ f64(table)[idx].T + f64(b1))
    h = relu(f64(w2).T @ h + f64(b2))
    e = f64(w3).T @ h + f64(b3)
    e0, e1 = e[:, :B], e[:, B:]
    t = f64(bw).reshape(D, D * D)
    p0 = (t.T @ e0).reshape(D, D, B)
    p1 = (t.T @ e1).reshape(D, D, B).transpose(1, 0, 2)
    z = (p0 * p1 * f64(bd)[:, :, None]).sum(axis=1) + f64(boff)
    return relu(f64(wc1).T @ z + f64(bc1))

@@ -1,0 +1,139 @@
+import concourse.mybir as mybir
+from concourse.masks import make_identity
+
+BF16, F32, U16 = mybir.dt.bfloat16, mybir.dt.float32, mybir.dt.uint16
+RELU = mybir.ActivationFunctionType.Relu
+IDENTITY = mybir.ActivationFunctionType.Identity
+MULT = mybir.AluOpType.mult
+
+P = 128
+GENES = 2048
+PAIRS = 512
+ENTRIES = 2 * PAIRS
+GENE_BLOCKS = GENES // P
+PAIR_BLOCKS = PAIRS // P
+BW_ROWS = 16
+BW_LOADS = P // BW_ROWS
+
+FLOPS = (
+    3 * 2 * P * P * ENTRIES
+    + 2 * 2 * P * P * P * PAIRS
+    + 3 * P * P * PAIRS
+    + 2 * P * P * PAIRS
+)
+
+
+def tile_recovermodel_b_kernel(
+    tc, table, w1, b1, w2, b2, w3, b3, bw, bd, boff, wc1, bc1, offs, out
+):
+    nc = tc.nc
+    with (
+        tc.tile_pool(name="held", bufs=1) as held,
+        tc.tile_pool(name="staged", bufs=BW_LOADS) as staged,
+        tc.tile_pool(name="work", bufs=4) as work,
+        tc.psum_pool(name="sums", bufs=1) as sums,
+        tc.psum_pool(name="banks", bufs=7) as banks,
+    ):
+        offsets = held.tile([P, ENTRIES // 16], U16, name="offsets")
+        nc.sync.dma_start(offsets[:], offs)
+
+        genes = held.tile([P, GENE_BLOCKS, P], BF16, name="genes")
+        nc.sync.dma_start(genes[:], table.rearrange("(a p) k -> p a k", p=P))
+
+        def load(source, shape, dtype, name):
+            loaded = held.tile(shape, dtype, name=name)
+            nc.scalar.dma_start(loaded[:], source)
+            return loaded
+
+        w1_sb = load(w1, [P, P], BF16, "w1_sb")
+        b1_sb = load(b1, [P, 1], F32, "b1_sb")
+        w2_sb = load(w2, [P, P], BF16, "w2_sb")
+        b2_sb = load(b2, [P, 1], F32, "b2_sb")
+        w3_sb = load(w3, [P, P], BF16, "w3_sb")
+        b3_sb = load(b3, [P, 1], F32, "b3_sb")
+        bd_sb = load(bd, [P, P], F32, "bd_sb")
+        boff_sb = load(boff, [P, 1], F32, "boff_sb")
+        wc1_sb = load(wc1, [P, P], BF16, "wc1_sb")
+        bc1_sb = load(bc1, [P, 1], F32, "bc1_sb")
+
+        bw_bf = held.tile([P, P, P], BF16, name="bw_bf")
+        for load_no in range(BW_LOADS):
+            rows = slice(load_no * BW_ROWS, (load_no + 1) * BW_ROWS)
+            bw_f32 = staged.tile([P, BW_ROWS, P], F32, name="bw_f32")
+            queue = nc.sync if load_no % 2 == 0 else nc.scalar
+            queue.dma_start(bw_f32[:], bw[:, rows, :])
+            nc.vector.tensor_copy(bw_bf[:, rows, :], bw_f32[:])
+
+        identity_bf = held.tile([P, P], BF16, name="identity_bf")
+        make_identity(nc, identity_bf[:])
+        identity_f32 = held.tile([P, P], F32, name="identity_f32")
+        make_identity(nc, identity_f32[:])
+
+        window = held.tile([P, GENES], BF16, name="window")
+        for group in range(GENE_BLOCKS // 4):
+            flipped = banks.tile([P, 4 * P], BF16, name="flipped", tag="bank")
+            for j in range(4):
+                nc.tensor.transpose(
+                    flipped[:, j * P : (j + 1) * P], genes[:, 4 * group + j, :], identity_bf[:]
+                )
+            nc.scalar.copy(window[:, group * 4 * P : (group + 1) * 4 * P], flipped[:])
+
+        bd_flipped = banks.tile([P, P], F32, name="bd_flipped", tag="bank")
+        nc.tensor.transpose(bd_flipped[:], bd_sb[:], identity_f32[:])
+        bd_t = held.tile([P, P], BF16, name="bd_t")
+        nc.scalar.copy(bd_t[:], bd_flipped[:])
+
+        halves = [slice(h * PAIRS, (h + 1) * PAIRS) for h in range(2)]
+        h1 = held.tile([P, ENTRIES], BF16, name="h1")
+        h2 = held.tile([P, ENTRIES], BF16, name="h2")
+        e = held.tile([P, ENTRIES], BF16, name="e")
+
+        looked_up = []
+        for h in range(2):
+            layer1 = banks.tile([P, PAIRS], F32, name="layer1", tag="bank")
+            piece = offsets[:, h * (PAIRS // 16) : (h + 1) * (PAIRS // 16)]
+            nc.tensor.matmul(layer1[:], w1_sb[:], window[:].indirect(piece), start=True, stop=True)
+            looked_up.append(layer1)
+        for h in range(2):
+            nc.scalar.activation(h1[:, halves[h]], looked_up[h][:], RELU, bias=b1_sb[:, 0:1])
+        for h in range(2):
+            layer2 = banks.tile([P, PAIRS], F32, name="layer2", tag="bank")
+            nc.tensor.matmul(layer2[:], w2_sb[:], h1[:, halves[h]], start=True, stop=True)
+            nc.scalar.activation(h2[:, halves[h]], layer2[:], RELU, bias=b2_sb[:, 0:1])
+        for h in range(2):
+            layer3 = banks.tile([P, PAIRS], F32, name="layer3", tag="bank")
+            nc.tensor.matmul(layer3[:], w3_sb[:], h2[:, halves[h]], start=True, stop=True)
+            nc.scalar.activation(e[:, halves[h]], layer3[:], IDENTITY, bias=b3_sb[:, 0:1])
+
+        z_t = sums.tile([P, PAIR_BLOCKS * P], F32, name="z_t")
+        for n in range(P):
+            u = banks.tile([P, PAIRS], F32, name="u", tag="bank")
+            nc.tensor.matmul(u[:], bw_bf[:, n, :], e[:, halves[0]], start=True, stop=True)
+            v = banks.tile([P, PAIRS], F32, name="v", tag="bank")
+            nc.tensor.matmul(v[:], bw_bf[:, :, n], e[:, halves[1]], start=True, stop=True)
+            u_sb = work.tile([P, PAIRS], F32, name="u_sb")
+            nc.scalar.copy(u_sb[:], u[:])
+            uv = work.tile([P, PAIRS], BF16, name="uv")
+            nc.vector.tensor_tensor(uv[:], v[:], u_sb[:], MULT)
+            for block in range(PAIR_BLOCKS):
+                nc.tensor.matmul(
+                    z_t[:, block * P + n : block * P + n + 1],
+                    uv[:, block * P : (block + 1) * P],
+                    bd_t[:, n : n + 1],
+                    start=True,
+                    stop=True,
+                )
+
+        z_t_sb = held.tile([P, PAIR_BLOCKS * P], F32, name="z_t_sb")
+        nc.vector.tensor_copy(z_t_sb[:], z_t[:])
+        z = banks.tile([P, PAIRS], F32, name="z", tag="bank")
+        for block in range(PAIR_BLOCKS):
+            columns = slice(block * P, (block + 1) * P)
+            nc.tensor.transpose(z[:, columns], z_t_sb[:, columns], identity_f32[:])
+        z_bf = held.tile([P, PAIRS], BF16, name="z_bf")
+        nc.scalar.activation(z_bf[:], z[:], IDENTITY, bias=boff_sb[:, 0:1])
+        combined = banks.tile([P, PAIRS], F32, name="combined", tag="bank")
+        nc.tensor.matmul(combined[:], wc1_sb[:], z_bf[:], start=True, stop=True)
+        out_sb = held.tile([P, PAIRS], F32, name="out_sb")
+        nc.scalar.activation(out_sb[:], combined[:], RELU, bias=bc1_sb[:, 0:1])
+        nc.sync.dma_start(out, out_sb[:])

@@ -11,7 +11,9 @@ GENES = 2048
 PAIRS = 512
 ENTRIES = 2 * PAIRS
 GENE_BLOCKS = GENES // P
-PAIR_BLOCKS = PAIRS // P
+QUADRANT = 32
+BATCH = 16
+LAG = 4
 BW_ROWS = 16
 BW_LOADS = P // BW_ROWS
 
@@ -31,6 +33,7 @@ def tile_recovermodel_b_kernel(
         tc.tile_pool(name="held", bufs=1) as held,
         tc.tile_pool(name="staged", bufs=BW_LOADS) as staged,
         tc.tile_pool(name="work", bufs=4) as work,
+        tc.tile_pool(name="products", bufs=BATCH + 2 * LAG) as products,
         tc.psum_pool(name="sums", bufs=1) as sums,
         tc.psum_pool(name="banks", bufs=7) as banks,
     ):
@@ -80,8 +83,10 @@ def tile_recovermodel_b_kernel(
 
         bd_flipped = banks.tile([P, P], F32, name="bd_flipped", tag="bank")
         nc.tensor.transpose(bd_flipped[:], bd_sb[:], identity_f32[:])
-        bd_t = held.tile([P, P], BF16, name="bd_t")
-        nc.scalar.copy(bd_t[:], bd_flipped[:])
+        pick = held.tile([P, P, QUADRANT], BF16, name="pick")
+        nc.gpsimd.memset(pick[:], 0.0)
+        diagonal = pick[:].rearrange("m (j r) c -> m j (r c)", r=QUADRANT)[:, :, :: QUADRANT + 1]
+        nc.vector.tensor_copy(diagonal, bd_flipped[:].rearrange("m (j r) -> m j r", r=QUADRANT))
 
         halves = [slice(h * PAIRS, (h + 1) * PAIRS) for h in range(2)]
         h1 = held.tile([P, ENTRIES], BF16, name="h1")
@@ -105,31 +110,36 @@ def tile_recovermodel_b_kernel(
             nc.tensor.matmul(layer3[:], w3_sb[:], h2[:, halves[h]], start=True, stop=True)
             nc.scalar.activation(e[:, halves[h]], layer3[:], IDENTITY, bias=b3_sb[:, 0:1])
 
-        z_t = sums.tile([P, PAIR_BLOCKS * P], F32, name="z_t")
-        for n in range(P):
-            u = banks.tile([P, PAIRS], F32, name="u", tag="bank")
-            nc.tensor.matmul(u[:], bw_bf[:, n, :], e[:, halves[0]], start=True, stop=True)
-            v = banks.tile([P, PAIRS], F32, name="v", tag="bank")
-            nc.tensor.matmul(v[:], bw_bf[:, :, n], e[:, halves[1]], start=True, stop=True)
-            u_sb = work.tile([P, PAIRS], F32, name="u_sb")
-            nc.scalar.copy(u_sb[:], u[:])
-            uv = work.tile([P, PAIRS], BF16, name="uv")
-            nc.vector.tensor_tensor(uv[:], v[:], u_sb[:], MULT)
-            for block in range(PAIR_BLOCKS):
+        z = sums.tile([P, PAIRS], F32, name="z")
+
+        def sum_over_m(batch):
+            for n, uv in batch:
+                rows = slice(n - n % QUADRANT, n - n % QUADRANT + QUADRANT)
                 nc.tensor.matmul(
-                    z_t[:, block * P + n : block * P + n + 1],
-                    uv[:, block * P : (block + 1) * P],
-                    bd_t[:, n : n + 1],
-                    start=True,
-                    stop=True,
+                    z[rows, :],
+                    pick[:, n, :],
+                    uv[:],
+                    start=(n % QUADRANT == 0),
+                    stop=(n % QUADRANT == QUADRANT - 1),
                 )
 
-        z_t_sb = held.tile([P, PAIR_BLOCKS * P], F32, name="z_t_sb")
-        nc.vector.tensor_copy(z_t_sb[:], z_t[:])
-        z = banks.tile([P, PAIRS], F32, name="z", tag="bank")
-        for block in range(PAIR_BLOCKS):
-            columns = slice(block * P, (block + 1) * P)
-            nc.tensor.transpose(z[:, columns], z_t_sb[:, columns], identity_f32[:])
+        order = [QUADRANT * j + r for r in range(QUADRANT) for j in range(P // QUADRANT)]
+        waiting = []
+        for n in order:
+            v = banks.tile([P, PAIRS], F32, name="v", tag="bank")
+            nc.tensor.matmul(v[:], bw_bf[:, :, n], e[:, halves[1]], start=True, stop=True)
+            u = banks.tile([P, PAIRS], F32, name="u", tag="bank")
+            nc.tensor.matmul(u[:], bw_bf[:, n, :], e[:, halves[0]], start=True, stop=True)
+            u_sb = work.tile([P, PAIRS], F32, name="u_sb")
+            nc.scalar.copy(u_sb[:], u[:])
+            uv = products.tile([P, PAIRS], BF16, name="uv")
+            nc.vector.tensor_tensor(uv[:], v[:], u_sb[:], MULT)
+            waiting.append((n, uv))
+            if len(waiting) == BATCH + LAG:
+                sum_over_m(waiting[:BATCH])
+                waiting = waiting[BATCH:]
+        sum_over_m(waiting)
+
         z_bf = held.tile([P, PAIRS], BF16, name="z_bf")
         nc.scalar.activation(z_bf[:], z[:], IDENTITY, bias=boff_sb[:, 0:1])
         combined = banks.tile([P, PAIRS], F32, name="combined", tag="bank")

@@ -4,6 +4,7 @@ from concourse.masks import make_identity
 BF16, F32, U16 = mybir.dt.bfloat16, mybir.dt.float32, mybir.dt.uint16
 RELU = mybir.ActivationFunctionType.Relu
 IDENTITY = mybir.ActivationFunctionType.Identity
+COPY = mybir.ActivationFunctionType.Copy
 MULT = mybir.AluOpType.mult
 
 P = 128
@@ -11,11 +12,13 @@ GENES = 2048
 PAIRS = 512
 ENTRIES = 2 * PAIRS
 GENE_BLOCKS = GENES // P
-QUADRANT = 32
-BATCH = 16
-LAG = 4
 BW_ROWS = 16
 BW_LOADS = P // BW_ROWS
+QUADRANT = 32
+QUADRANTS = P // QUADRANT
+BATCH = 16
+LAG = 4
+AHEAD = 24
 
 FLOPS = (
     3 * 2 * P * P * ENTRIES
@@ -32,7 +35,7 @@ def tile_recovermodel_b_kernel(
     with (
         tc.tile_pool(name="held", bufs=1) as held,
         tc.tile_pool(name="staged", bufs=BW_LOADS) as staged,
-        tc.tile_pool(name="work", bufs=4) as work,
+        tc.tile_pool(name="copies", bufs=AHEAD + 2) as copies,
         tc.tile_pool(name="products", bufs=BATCH + 2 * LAG) as products,
         tc.psum_pool(name="sums", bufs=1) as sums,
         tc.psum_pool(name="banks", bufs=7) as banks,
@@ -43,29 +46,33 @@ def tile_recovermodel_b_kernel(
         genes = held.tile([P, GENE_BLOCKS, P], BF16, name="genes")
         nc.sync.dma_start(genes[:], table.rearrange("(a p) k -> p a k", p=P))
 
-        def load(source, shape, dtype, name):
+        def load(queue, source, shape, dtype, name):
             loaded = held.tile(shape, dtype, name=name)
-            nc.scalar.dma_start(loaded[:], source)
+            queue.dma_start(loaded[:], source)
             return loaded
 
-        w1_sb = load(w1, [P, P], BF16, "w1_sb")
-        b1_sb = load(b1, [P, 1], F32, "b1_sb")
-        w2_sb = load(w2, [P, P], BF16, "w2_sb")
-        b2_sb = load(b2, [P, 1], F32, "b2_sb")
-        w3_sb = load(w3, [P, P], BF16, "w3_sb")
-        b3_sb = load(b3, [P, 1], F32, "b3_sb")
-        bd_sb = load(bd, [P, P], F32, "bd_sb")
-        boff_sb = load(boff, [P, 1], F32, "boff_sb")
-        wc1_sb = load(wc1, [P, P], BF16, "wc1_sb")
-        bc1_sb = load(bc1, [P, 1], F32, "bc1_sb")
+        w1_sb = load(nc.scalar, w1, [P, P], BF16, "w1_sb")
+        b1_sb = load(nc.scalar, b1, [P, 1], F32, "b1_sb")
+        w2_sb = load(nc.scalar, w2, [P, P], BF16, "w2_sb")
+        b2_sb = load(nc.scalar, b2, [P, 1], F32, "b2_sb")
+        w3_sb = load(nc.scalar, w3, [P, P], BF16, "w3_sb")
+        b3_sb = load(nc.scalar, b3, [P, 1], F32, "b3_sb")
 
         bw_bf = held.tile([P, P, P], BF16, name="bw_bf")
         for load_no in range(BW_LOADS):
             rows = slice(load_no * BW_ROWS, (load_no + 1) * BW_ROWS)
             bw_f32 = staged.tile([P, BW_ROWS, P], F32, name="bw_f32")
-            queue = nc.sync if load_no % 2 == 0 else nc.scalar
-            queue.dma_start(bw_f32[:], bw[:, rows, :])
+            nc.sync.dma_start(bw_f32[:], bw[:, rows, :])
             nc.vector.tensor_copy(bw_bf[:, rows, :], bw_f32[:])
+
+        bd_sb = load(nc.sync, bd, [P, P], F32, "bd_sb")
+        bc1_sb = load(nc.sync, bc1, [P, 1], F32, "bc1_sb")
+        wc1_sb = held.tile([P, P], BF16, name="wc1_sb")
+        boff_sb = held.tile([P, 1], F32, name="boff_sb")
+        for j in range(QUADRANTS):
+            rows = slice(j * QUADRANT, (j + 1) * QUADRANT)
+            nc.sync.dma_start(wc1_sb[rows, :], wc1.rearrange("(r j) c -> j r c", j=QUADRANTS)[j])
+            nc.sync.dma_start(boff_sb[rows, :], boff.rearrange("(r j) o -> j r o", j=QUADRANTS)[j])
 
         identity_bf = held.tile([P, P], BF16, name="identity_bf")
         make_identity(nc, identity_bf[:])
@@ -79,14 +86,7 @@ def tile_recovermodel_b_kernel(
                 nc.tensor.transpose(
                     flipped[:, j * P : (j + 1) * P], genes[:, 4 * group + j, :], identity_bf[:]
                 )
-            nc.scalar.copy(window[:, group * 4 * P : (group + 1) * 4 * P], flipped[:])
-
-        bd_flipped = banks.tile([P, P], F32, name="bd_flipped", tag="bank")
-        nc.tensor.transpose(bd_flipped[:], bd_sb[:], identity_f32[:])
-        pick = held.tile([P, P, QUADRANT], BF16, name="pick")
-        nc.gpsimd.memset(pick[:], 0.0)
-        diagonal = pick[:].rearrange("m (j r) c -> m j (r c)", r=QUADRANT)[:, :, :: QUADRANT + 1]
-        nc.vector.tensor_copy(diagonal, bd_flipped[:].rearrange("m (j r) -> m j r", r=QUADRANT))
+            nc.vector.tensor_copy(window[:, group * 4 * P : (group + 1) * 4 * P], flipped[:])
 
         halves = [slice(h * PAIRS, (h + 1) * PAIRS) for h in range(2)]
         h1 = held.tile([P, ENTRIES], BF16, name="h1")
@@ -114,26 +114,45 @@ def tile_recovermodel_b_kernel(
 
         def sum_over_m(batch):
             for n, uv in batch:
-                rows = slice(n - n % QUADRANT, n - n % QUADRANT + QUADRANT)
+                j, r = n % QUADRANTS, n // QUADRANTS
                 nc.tensor.matmul(
-                    z[rows, :],
+                    z[j * QUADRANT : (j + 1) * QUADRANT, :],
                     pick[:, n, :],
                     uv[:],
-                    start=(n % QUADRANT == 0),
-                    stop=(n % QUADRANT == QUADRANT - 1),
+                    start=(r == 0),
+                    stop=(r == QUADRANT - 1),
                 )
 
-        order = [QUADRANT * j + r for r in range(QUADRANT) for j in range(P // QUADRANT)]
-        waiting = []
-        for n in order:
-            v = banks.tile([P, PAIRS], F32, name="v", tag="bank")
-            nc.tensor.matmul(v[:], bw_bf[:, :, n], e[:, halves[1]], start=True, stop=True)
+        u_copies = []
+
+        def make_next_u():
+            n = len(u_copies)
             u = banks.tile([P, PAIRS], F32, name="u", tag="bank")
             nc.tensor.matmul(u[:], bw_bf[:, n, :], e[:, halves[0]], start=True, stop=True)
-            u_sb = work.tile([P, PAIRS], F32, name="u_sb")
+            u_sb = copies.tile([P, PAIRS], F32, name="u_sb")
             nc.scalar.copy(u_sb[:], u[:])
+            u_copies.append(u_sb)
+
+        for n in range(AHEAD):
+            make_next_u()
+
+        bd_flipped = banks.tile([P, P], F32, name="bd_flipped", tag="bank")
+        nc.tensor.transpose(bd_flipped[:], bd_sb[:], identity_f32[:])
+        pick = held.tile([P, P, QUADRANT], BF16, name="pick")
+        nc.gpsimd.memset(pick[:], 0.0)
+        pick_flat = pick[:].rearrange("m n c -> m (n c)")
+        for j in range(QUADRANTS):
+            places = pick_flat[:, j * QUADRANT :: QUADRANTS * QUADRANT + 1]
+            nc.scalar.activation(places, bd_flipped[:, j::QUADRANTS], COPY)
+
+        waiting = []
+        for n in range(P):
+            while len(u_copies) < min(P, n + 1 + AHEAD * (P - n) // P):
+                make_next_u()
+            v = banks.tile([P, PAIRS], F32, name="v", tag="bank")
+            nc.tensor.matmul(v[:], bw_bf[:, :, n], e[:, halves[1]], start=True, stop=True)
             uv = products.tile([P, PAIRS], BF16, name="uv")
-            nc.vector.tensor_tensor(uv[:], v[:], u_sb[:], MULT)
+            nc.vector.tensor_tensor(uv[:], v[:], u_copies[n][:], MULT)
             waiting.append((n, uv))
             if len(waiting) == BATCH + LAG:
                 sum_over_m(waiting[:BATCH])

@@ -4,7 +4,6 @@ from concourse.masks import make_identity
 BF16, F32, U16 = mybir.dt.bfloat16, mybir.dt.float32, mybir.dt.uint16
 RELU = mybir.ActivationFunctionType.Relu
 IDENTITY = mybir.ActivationFunctionType.Identity
-COPY = mybir.ActivationFunctionType.Copy
 MULT = mybir.AluOpType.mult
 
 P = 128
@@ -14,11 +13,14 @@ ENTRIES = 2 * PAIRS
 GENE_BLOCKS = GENES // P
 BW_ROWS = 16
 BW_LOADS = P // BW_ROWS
+BANK_BLOCKS = 8
+GROUP = 4
+GROUPS = P // GROUP
 QUADRANT = 32
 QUADRANTS = P // QUADRANT
 BATCH = 16
 LAG = 4
-AHEAD = 24
+SHARE = 4
 
 FLOPS = (
     3 * 2 * P * P * ENTRIES
@@ -35,10 +37,13 @@ def tile_recovermodel_b_kernel(
     with (
         tc.tile_pool(name="held", bufs=1) as held,
         tc.tile_pool(name="staged", bufs=BW_LOADS) as staged,
-        tc.tile_pool(name="copies", bufs=AHEAD + 2) as copies,
+        tc.tile_pool(name="flips", bufs=3) as flips,
+        tc.tile_pool(name="forms", bufs=4) as forms,
+        tc.tile_pool(name="moved", bufs=3) as moved,
         tc.tile_pool(name="products", bufs=BATCH + 2 * LAG) as products,
         tc.psum_pool(name="sums", bufs=1) as sums,
-        tc.psum_pool(name="banks", bufs=7) as banks,
+        tc.psum_pool(name="blocks", bufs=2) as blocks,
+        tc.psum_pool(name="banks", bufs=5) as banks,
     ):
         offsets = held.tile([P, ENTRIES // 16], U16, name="offsets")
         nc.sync.dma_start(offsets[:], offs)
@@ -51,6 +56,8 @@ def tile_recovermodel_b_kernel(
             queue.dma_start(loaded[:], source)
             return loaded
 
+        bd_sb = load(nc.sync, bd, [P, P], F32, "bd_sb")
+
         w1_sb = load(nc.scalar, w1, [P, P], BF16, "w1_sb")
         b1_sb = load(nc.scalar, b1, [P, 1], F32, "b1_sb")
         w2_sb = load(nc.scalar, w2, [P, P], BF16, "w2_sb")
@@ -58,33 +65,35 @@ def tile_recovermodel_b_kernel(
         w3_sb = load(nc.scalar, w3, [P, P], BF16, "w3_sb")
         b3_sb = load(nc.scalar, b3, [P, 1], F32, "b3_sb")
 
-        bw_bf = held.tile([P, P, P], BF16, name="bw_bf")
+        bw_staged = []
         for load_no in range(BW_LOADS):
-            rows = slice(load_no * BW_ROWS, (load_no + 1) * BW_ROWS)
             bw_f32 = staged.tile([P, BW_ROWS, P], F32, name="bw_f32")
-            nc.sync.dma_start(bw_f32[:], bw[:, rows, :])
-            nc.vector.tensor_copy(bw_bf[:, rows, :], bw_f32[:])
+            nc.sync.dma_start(bw_f32[:], bw[:, load_no * BW_ROWS : (load_no + 1) * BW_ROWS, :])
+            bw_staged.append(bw_f32)
 
-        bd_sb = load(nc.sync, bd, [P, P], F32, "bd_sb")
         bc1_sb = load(nc.sync, bc1, [P, 1], F32, "bc1_sb")
         wc1_sb = held.tile([P, P], BF16, name="wc1_sb")
         boff_sb = held.tile([P, 1], F32, name="boff_sb")
-        for j in range(QUADRANTS):
-            rows = slice(j * QUADRANT, (j + 1) * QUADRANT)
-            nc.sync.dma_start(wc1_sb[rows, :], wc1.rearrange("(r j) c -> j r c", j=QUADRANTS)[j])
-            nc.sync.dma_start(boff_sb[rows, :], boff.rearrange("(r j) o -> j r o", j=QUADRANTS)[j])
+        for q in range(QUADRANTS):
+            rows = slice(q * QUADRANT, (q + 1) * QUADRANT)
+            nc.sync.dma_start(wc1_sb[rows, :], wc1.rearrange("(r q) c -> q r c", q=QUADRANTS)[q])
+            nc.sync.dma_start(boff_sb[rows, :], boff.rearrange("(r q) o -> q r o", q=QUADRANTS)[q])
 
         identity_bf = held.tile([P, P], BF16, name="identity_bf")
         make_identity(nc, identity_bf[:])
         identity_f32 = held.tile([P, P], F32, name="identity_f32")
         make_identity(nc, identity_f32[:])
 
+        pick = held.tile([P, QUADRANT, QUADRANT], BF16, name="pick")
+        nc.gpsimd.memset(pick[:], 0.0)
+        nc.gpsimd.memset(pick[:].rearrange("k r c -> k (r c)")[:, :: QUADRANT + 1], 1.0)
+
         window = held.tile([P, GENES], BF16, name="window")
         for group in range(GENE_BLOCKS // 4):
             flipped = banks.tile([P, 4 * P], BF16, name="flipped", tag="bank")
-            for j in range(4):
+            for a in range(4):
                 nc.tensor.transpose(
-                    flipped[:, j * P : (j + 1) * P], genes[:, 4 * group + j, :], identity_bf[:]
+                    flipped[:, a * P : (a + 1) * P], genes[:, 4 * group + a, :], identity_bf[:]
                 )
             nc.vector.tensor_copy(window[:, group * 4 * P : (group + 1) * 4 * P], flipped[:])
 
@@ -110,54 +119,94 @@ def tile_recovermodel_b_kernel(
             nc.tensor.matmul(layer3[:], w3_sb[:], h2[:, halves[h]], start=True, stop=True)
             nc.scalar.activation(e[:, halves[h]], layer3[:], IDENTITY, bias=b3_sb[:, 0:1])
 
+        bd_bank = banks.tile([P, P], F32, name="bd_bank", tag="bank")
+        nc.tensor.transpose(bd_bank[:], bd_sb[:], identity_f32[:])
+        bd_flipped = held.tile([P, P], F32, name="bd_flipped")
+        nc.vector.tensor_copy(bd_flipped[:], bd_bank[:])
+
+        bw_bf = held.tile([P, P, P], BF16, name="bw_bf")
+        rows_flipped = held.tile([P, P, P], BF16, name="rows_flipped")
+
+        def flip_rows(load_no, copy):
+            for first in range(load_no * BW_ROWS, (load_no + 1) * BW_ROWS, BANK_BLOCKS):
+                bank = banks.tile([P, BANK_BLOCKS, P], BF16, name="rows_bank", tag="bank")
+                for i in range(BANK_BLOCKS):
+                    nc.tensor.transpose(bank[:, i, :], bw_bf[:, first + i, :], identity_bf[:])
+                copy(rows_flipped[:, first : first + BANK_BLOCKS, :], bank[:])
+
+        for load_no in range(BW_LOADS):
+            rows = slice(load_no * BW_ROWS, (load_no + 1) * BW_ROWS)
+            nc.vector.tensor_copy(bw_bf[:, rows, :], bw_staged[load_no][:])
+            if load_no < BW_LOADS - 1:
+                flip_rows(load_no, nc.scalar.copy)
+
+        def flip_columns(group):
+            bank = blocks.tile([P, BANK_BLOCKS, P], BF16, name="columns_bank", tag="block")
+            for i in range(GROUP):
+                nc.tensor.transpose(bank[:, i, :], bw_bf[:, :, group * GROUP + i], identity_bf[:])
+            columns_flipped = flips.tile([P, GROUP, P], BF16, name="columns_flipped")
+            for i in reversed(range(GROUP)):
+                n = group * GROUP + i
+                nc.scalar.activation(
+                    columns_flipped[:, i, :], bank[:, i, :], IDENTITY, scale=bd_flipped[:, n : n + 1]
+                )
+            return columns_flipped
+
+        def make_forms(group, columns_flipped):
+            bank = blocks.tile([P, BANK_BLOCKS, P], BF16, name="forms_bank", tag="block")
+            for i in range(GROUP):
+                nc.tensor.matmul(
+                    bank[:, i, :],
+                    columns_flipped[:, i, :],
+                    rows_flipped[:, group * GROUP + i, :],
+                    start=True,
+                    stop=True,
+                )
+            form = forms.tile([P, GROUP, P], BF16, name="form")
+            nc.scalar.copy(form[:], bank[:, :GROUP, :])
+            return form
+
         z = sums.tile([P, PAIRS], F32, name="z")
 
-        def sum_over_m(batch):
-            for n, uv in batch:
-                j, r = n % QUADRANTS, n // QUADRANTS
+        def sum_over_k(batch):
+            for n, product in batch:
+                q, r = n % QUADRANTS, n // QUADRANTS
                 nc.tensor.matmul(
-                    z[j * QUADRANT : (j + 1) * QUADRANT, :],
-                    pick[:, n, :],
-                    uv[:],
+                    z[q * QUADRANT : (q + 1) * QUADRANT, :],
+                    pick[:, r, :],
+                    product[:],
                     start=(r == 0),
                     stop=(r == QUADRANT - 1),
                 )
 
-        u_copies = []
-
-        def make_next_u():
-            n = len(u_copies)
-            u = banks.tile([P, PAIRS], F32, name="u", tag="bank")
-            nc.tensor.matmul(u[:], bw_bf[:, n, :], e[:, halves[0]], start=True, stop=True)
-            u_sb = copies.tile([P, PAIRS], F32, name="u_sb")
-            nc.scalar.copy(u_sb[:], u[:])
-            u_copies.append(u_sb)
-
-        for n in range(AHEAD):
-            make_next_u()
-
-        bd_flipped = banks.tile([P, P], F32, name="bd_flipped", tag="bank")
-        nc.tensor.transpose(bd_flipped[:], bd_sb[:], identity_f32[:])
-        pick = held.tile([P, P, QUADRANT], BF16, name="pick")
-        nc.gpsimd.memset(pick[:], 0.0)
-        pick_flat = pick[:].rearrange("m n c -> m (n c)")
-        for j in range(QUADRANTS):
-            places = pick_flat[:, j * QUADRANT :: QUADRANTS * QUADRANT + 1]
-            nc.scalar.activation(places, bd_flipped[:, j::QUADRANTS], COPY)
-
+        flipped_of = {0: flip_columns(0), 1: flip_columns(1)}
+        flip_rows(BW_LOADS - 1, nc.vector.tensor_copy)
+        form_of = {0: make_forms(0, flipped_of[0])}
+        flipped_of[2] = flip_columns(2)
+        form_of[1] = make_forms(1, flipped_of[1])
         waiting = []
-        for n in range(P):
-            while len(u_copies) < min(P, n + 1 + AHEAD * (P - n) // P):
-                make_next_u()
-            v = banks.tile([P, PAIRS], F32, name="v", tag="bank")
-            nc.tensor.matmul(v[:], bw_bf[:, :, n], e[:, halves[1]], start=True, stop=True)
-            uv = products.tile([P, PAIRS], BF16, name="uv")
-            nc.vector.tensor_tensor(uv[:], v[:], u_copies[n][:], MULT)
-            waiting.append((n, uv))
-            if len(waiting) == BATCH + LAG:
-                sum_over_m(waiting[:BATCH])
-                waiting = waiting[BATCH:]
-        sum_over_m(waiting)
+        for group in range(GROUPS):
+            form = form_of[group]
+            for i in range(GROUP):
+                if i == GROUP // 2 and group + 2 < GROUPS:
+                    form_of[group + 2] = make_forms(group + 2, flipped_of[group + 2])
+                if i == GROUP // 2 and group + 3 < GROUPS:
+                    flipped_of[group + 3] = flip_columns(group + 3)
+                n = group * GROUP + i
+                half_done = banks.tile([P, PAIRS], F32, name="half_done", tag="bank")
+                nc.tensor.matmul(half_done[:], form[:, i, :], e[:, halves[1]], start=True, stop=True)
+                product = products.tile([P, PAIRS], BF16, name="product")
+                if n % SHARE == 0:
+                    half_moved = moved.tile([P, PAIRS], F32, name="half_moved")
+                    nc.scalar.copy(half_moved[:], half_done[:])
+                    nc.gpsimd.tensor_tensor(product[:], half_moved[:], e[:, halves[0]], MULT)
+                else:
+                    nc.vector.tensor_tensor(product[:], half_done[:], e[:, halves[0]], MULT)
+                waiting.append((n, product))
+                if len(waiting) == BATCH + LAG:
+                    sum_over_k(waiting[:BATCH])
+                    waiting = waiting[BATCH:]
+        sum_over_k(waiting)
 
         z_bf = held.tile([P, PAIRS], BF16, name="z_bf")
         nc.scalar.activation(z_bf[:], z[:], IDENTITY, bias=boff_sb[:, 0:1])

@@ -19,7 +19,7 @@ GROUPS = P // GROUP
 QUADRANT = 32
 QUADRANTS = P // QUADRANT
 BATCH = 16
-LAG = 4
+LAG = 8
 SHARE = 4
 
 FLOPS = (
@@ -127,29 +127,34 @@ def tile_recovermodel_b_kernel(
         bw_bf = held.tile([P, P, P], BF16, name="bw_bf")
         rows_flipped = held.tile([P, P, P], BF16, name="rows_flipped")
 
-        def flip_rows(load_no, copy):
-            for first in range(load_no * BW_ROWS, (load_no + 1) * BW_ROWS, BANK_BLOCKS):
+        def weigh_on_scalar(weighted, block, weights):
+            nc.scalar.activation(weighted, block, IDENTITY, scale=weights)
+
+        def weigh_on_vector(weighted, block, weights):
+            nc.vector.tensor_scalar(weighted, block, weights, None, MULT)
+
+        def flip_rows(load_no, weighers):
+            for bank_no, weigh in enumerate(weighers):
+                first = load_no * BW_ROWS + bank_no * BANK_BLOCKS
                 bank = banks.tile([P, BANK_BLOCKS, P], BF16, name="rows_bank", tag="bank")
                 for i in range(BANK_BLOCKS):
                     nc.tensor.transpose(bank[:, i, :], bw_bf[:, first + i, :], identity_bf[:])
-                copy(rows_flipped[:, first : first + BANK_BLOCKS, :], bank[:])
+                for i in range(BANK_BLOCKS):
+                    n = first + i
+                    weigh(rows_flipped[:, n, :], bank[:, i, :], bd_flipped[:, n : n + 1])
 
         for load_no in range(BW_LOADS):
             rows = slice(load_no * BW_ROWS, (load_no + 1) * BW_ROWS)
             nc.vector.tensor_copy(bw_bf[:, rows, :], bw_staged[load_no][:])
             if load_no < BW_LOADS - 1:
-                flip_rows(load_no, nc.scalar.copy)
+                flip_rows(load_no, [weigh_on_scalar, weigh_on_vector])
 
         def flip_columns(group):
             bank = blocks.tile([P, BANK_BLOCKS, P], BF16, name="columns_bank", tag="block")
             for i in range(GROUP):
                 nc.tensor.transpose(bank[:, i, :], bw_bf[:, :, group * GROUP + i], identity_bf[:])
             columns_flipped = flips.tile([P, GROUP, P], BF16, name="columns_flipped")
-            for i in reversed(range(GROUP)):
-                n = group * GROUP + i
-                nc.scalar.activation(
-                    columns_flipped[:, i, :], bank[:, i, :], IDENTITY, scale=bd_flipped[:, n : n + 1]
-                )
+            nc.scalar.copy(columns_flipped[:], bank[:, :GROUP, :])
             return columns_flipped
 
         def make_forms(group, columns_flipped):
@@ -180,10 +185,10 @@ def tile_recovermodel_b_kernel(
                 )
 
         flipped_of = {0: flip_columns(0), 1: flip_columns(1)}
-        flip_rows(BW_LOADS - 1, nc.vector.tensor_copy)
         form_of = {0: make_forms(0, flipped_of[0])}
         flipped_of[2] = flip_columns(2)
         form_of[1] = make_forms(1, flipped_of[1])
+        flip_rows(BW_LOADS - 1, [weigh_on_vector, weigh_on_vector])
         waiting = []
         for group in range(GROUPS):
             form = form_of[group]

@@ -16,6 +16,9 @@ BW_LOADS = P // BW_ROWS
 BANK_BLOCKS = 8
 GROUP = 4
 GROUPS = P // GROUP
+LATE = P // 2
+LATE_ROWS = 32
+LATE_LOADS = P // LATE_ROWS
 QUADRANT = 32
 QUADRANTS = P // QUADRANT
 BATCH = 16
@@ -67,9 +70,16 @@ def tile_recovermodel_b_kernel(
 
         bw_staged = []
         for load_no in range(BW_LOADS):
-            bw_f32 = staged.tile([P, BW_ROWS, P], F32, name="bw_f32")
+            bw_f32 = staged.tile([P, BW_ROWS, P], F32, name="bw_f32", tag="bw_f32")
             nc.sync.dma_start(bw_f32[:], bw[:, load_no * BW_ROWS : (load_no + 1) * BW_ROWS, :])
             bw_staged.append(bw_f32)
+
+        late_staged = []
+        for load_no in range(LATE_LOADS):
+            rows = slice(load_no * LATE_ROWS, (load_no + 1) * LATE_ROWS)
+            late_f32 = staged.tile([P, LATE_ROWS, P - LATE], F32, name="late_f32", tag="bw_f32")
+            nc.sync.dma_start(late_f32[:], bw[rows, :, LATE:].rearrange("j m n -> m j n"))
+            late_staged.append(late_f32)
 
         bc1_sb = load(nc.sync, bc1, [P, 1], F32, "bc1_sb")
         wc1_sb = held.tile([P, P], BF16, name="wc1_sb")
@@ -157,13 +167,20 @@ def tile_recovermodel_b_kernel(
             nc.scalar.copy(columns_flipped[:], bank[:, :GROUP, :])
             return columns_flipped
 
-        def make_forms(group, columns_flipped):
+        columns_late = held.tile([P, P, P - LATE], BF16, name="columns_late")
+
+        def round_late_columns(load_no):
+            rows = slice(load_no * LATE_ROWS, (load_no + 1) * LATE_ROWS)
+            nc.scalar.copy(columns_late[:, rows, :], late_staged[load_no][:])
+
+        def make_forms(group):
             bank = blocks.tile([P, BANK_BLOCKS, P], BF16, name="forms_bank", tag="block")
             for i in range(GROUP):
+                n = group * GROUP + i
                 nc.tensor.matmul(
                     bank[:, i, :],
-                    columns_flipped[:, i, :],
-                    rows_flipped[:, group * GROUP + i, :],
+                    flipped_of[group][:, i, :] if n < LATE else columns_late[:, :, n - LATE],
+                    rows_flipped[:, n, :],
                     start=True,
                     stop=True,
                 )
@@ -185,17 +202,20 @@ def tile_recovermodel_b_kernel(
                 )
 
         flipped_of = {0: flip_columns(0), 1: flip_columns(1)}
-        form_of = {0: make_forms(0, flipped_of[0])}
+        form_of = {0: make_forms(0)}
         flipped_of[2] = flip_columns(2)
-        form_of[1] = make_forms(1, flipped_of[1])
+        form_of[1] = make_forms(1)
         flip_rows(BW_LOADS - 1, [weigh_on_vector, weigh_on_vector])
+        first_late_use = LATE // GROUP - 2
         waiting = []
         for group in range(GROUPS):
             form = form_of[group]
+            if first_late_use - LATE_LOADS <= group < first_late_use:
+                round_late_columns(group - (first_late_use - LATE_LOADS))
             for i in range(GROUP):
                 if i == GROUP // 2 and group + 2 < GROUPS:
-                    form_of[group + 2] = make_forms(group + 2, flipped_of[group + 2])
-                if i == GROUP // 2 and group + 3 < GROUPS:
+                    form_of[group + 2] = make_forms(group + 2)
+                if i == GROUP // 2 and (group + 3) * GROUP < LATE:
                     flipped_of[group + 3] = flip_columns(group + 3)
                 n = group * GROUP + i
                 half_done = banks.tile([P, PAIRS], F32, name="half_done", tag="bank")

@@ -11,17 +11,17 @@ GENES = 2048
 PAIRS = 512
 ENTRIES = 2 * PAIRS
 GENE_BLOCKS = GENES // P
-BW_ROWS = 16
+BW_ROWS = 8
 BW_LOADS = P // BW_ROWS
-BANK_BLOCKS = 8
 GROUP = 4
 GROUPS = P // GROUP
-LATE = P // 2
-LATE_ROWS = 32
+LEAD = 2
+LATE_ROWS = 8
 LATE_LOADS = P // LATE_ROWS
+LATE = (LATE_LOADS + LEAD) * GROUP
 QUADRANT = 32
 QUADRANTS = P // QUADRANT
-BATCH = 16
+BATCH = 32
 LAG = 8
 SHARE = 4
 
@@ -40,8 +40,7 @@ def tile_recovermodel_b_kernel(
     with (
         tc.tile_pool(name="held", bufs=1) as held,
         tc.tile_pool(name="staged", bufs=BW_LOADS) as staged,
-        tc.tile_pool(name="flips", bufs=3) as flips,
-        tc.tile_pool(name="forms", bufs=4) as forms,
+        tc.tile_pool(name="aheads", bufs=2 * LEAD) as aheads,
         tc.tile_pool(name="moved", bufs=3) as moved,
         tc.tile_pool(name="products", bufs=BATCH + 2 * LAG) as products,
         tc.psum_pool(name="sums", bufs=1) as sums,
@@ -143,50 +142,22 @@ def tile_recovermodel_b_kernel(
         def weigh_on_vector(weighted, block, weights):
             nc.vector.tensor_scalar(weighted, block, weights, None, MULT)
 
-        def flip_rows(load_no, weighers):
-            for bank_no, weigh in enumerate(weighers):
-                first = load_no * BW_ROWS + bank_no * BANK_BLOCKS
-                bank = banks.tile([P, BANK_BLOCKS, P], BF16, name="rows_bank", tag="bank")
-                for i in range(BANK_BLOCKS):
-                    nc.tensor.transpose(bank[:, i, :], bw_bf[:, first + i, :], identity_bf[:])
-                for i in range(BANK_BLOCKS):
-                    n = first + i
-                    weigh(rows_flipped[:, n, :], bank[:, i, :], bd_flipped[:, n : n + 1])
-
         for load_no in range(BW_LOADS):
             rows = slice(load_no * BW_ROWS, (load_no + 1) * BW_ROWS)
             nc.vector.tensor_copy(bw_bf[:, rows, :], bw_staged[load_no][:])
-            if load_no < BW_LOADS - 1:
-                flip_rows(load_no, [weigh_on_scalar, weigh_on_vector])
-
-        def flip_columns(group):
-            bank = blocks.tile([P, BANK_BLOCKS, P], BF16, name="columns_bank", tag="block")
-            for i in range(GROUP):
-                nc.tensor.transpose(bank[:, i, :], bw_bf[:, :, group * GROUP + i], identity_bf[:])
-            columns_flipped = flips.tile([P, GROUP, P], BF16, name="columns_flipped")
-            nc.scalar.copy(columns_flipped[:], bank[:, :GROUP, :])
-            return columns_flipped
+            bank = banks.tile([P, BW_ROWS, P], BF16, name="rows_bank", tag="bank")
+            for i in range(BW_ROWS):
+                nc.tensor.transpose(bank[:, i, :], bw_bf[:, load_no * BW_ROWS + i, :], identity_bf[:])
+            weigh = weigh_on_scalar if load_no % 2 == 0 else weigh_on_vector
+            for i in range(BW_ROWS):
+                n = load_no * BW_ROWS + i
+                weigh(rows_flipped[:, n, :], bank[:, i, :], bd_flipped[:, n : n + 1])
 
         columns_late = held.tile([P, P, P - LATE], BF16, name="columns_late")
 
         def round_late_columns(load_no):
             rows = slice(load_no * LATE_ROWS, (load_no + 1) * LATE_ROWS)
             nc.scalar.copy(columns_late[:, rows, :], late_staged[load_no][:])
-
-        def make_forms(group):
-            bank = blocks.tile([P, BANK_BLOCKS, P], BF16, name="forms_bank", tag="block")
-            for i in range(GROUP):
-                n = group * GROUP + i
-                nc.tensor.matmul(
-                    bank[:, i, :],
-                    flipped_of[group][:, i, :] if n < LATE else columns_late[:, :, n - LATE],
-                    rows_flipped[:, n, :],
-                    start=True,
-                    stop=True,
-                )
-            form = forms.tile([P, GROUP, P], BF16, name="form")
-            nc.scalar.copy(form[:], bank[:, :GROUP, :])
-            return form
 
         z = sums.tile([P, PAIRS], F32, name="z")
 
@@ -201,36 +172,55 @@ def tile_recovermodel_b_kernel(
                     stop=(r == QUADRANT - 1),
                 )
 
-        flipped_of = {0: flip_columns(0), 1: flip_columns(1)}
-        form_of = {0: make_forms(0)}
-        flipped_of[2] = flip_columns(2)
-        form_of[1] = make_forms(1)
-        flip_rows(BW_LOADS - 1, [weigh_on_vector, weigh_on_vector])
-        first_late_use = LATE // GROUP - 2
+        COLUMNS, FORMS = 0, 1
+        ahead_of = {}
         waiting = []
-        for group in range(GROUPS):
-            form = form_of[group]
-            if first_late_use - LATE_LOADS <= group < first_late_use:
-                round_late_columns(group - (first_late_use - LATE_LOADS))
+        for group in range(-2 * LEAD, GROUPS):
+            flips = 0 <= (group + 2 * LEAD) * GROUP < LATE
+            makes = 0 <= group + LEAD < GROUPS
+            if flips or makes:
+                bank = blocks.tile([P, 2, GROUP, P], BF16, name="ahead_bank")
+            if 0 <= group < LATE_LOADS:
+                round_late_columns(group)
             for i in range(GROUP):
-                if i == GROUP // 2 and group + 2 < GROUPS:
-                    form_of[group + 2] = make_forms(group + 2)
-                if i == GROUP // 2 and (group + 3) * GROUP < LATE:
-                    flipped_of[group + 3] = flip_columns(group + 3)
                 n = group * GROUP + i
-                half_done = banks.tile([P, PAIRS], F32, name="half_done", tag="bank")
-                nc.tensor.matmul(half_done[:], form[:, i, :], e[:, halves[1]], start=True, stop=True)
-                product = products.tile([P, PAIRS], BF16, name="product")
-                if n % SHARE == 0:
-                    half_moved = moved.tile([P, PAIRS], F32, name="half_moved")
-                    nc.scalar.copy(half_moved[:], half_done[:])
-                    nc.gpsimd.tensor_tensor(product[:], half_moved[:], e[:, halves[0]], MULT)
-                else:
-                    nc.vector.tensor_tensor(product[:], half_done[:], e[:, halves[0]], MULT)
-                waiting.append((n, product))
-                if len(waiting) == BATCH + LAG:
-                    sum_over_k(waiting[:BATCH])
-                    waiting = waiting[BATCH:]
+                n_made = n + LEAD * GROUP
+                n_flipped = n + 2 * LEAD * GROUP
+                if group >= 0:
+                    half_done = banks.tile([P, PAIRS], F32, name="half_done", tag="bank")
+                    nc.tensor.matmul(
+                        half_done[:],
+                        ahead_of[group - LEAD][:, FORMS, i, :],
+                        e[:, halves[1]],
+                        start=True,
+                        stop=True,
+                    )
+                    product = products.tile([P, PAIRS], BF16, name="product")
+                    if n % SHARE == 0:
+                        half_moved = moved.tile([P, PAIRS], F32, name="half_moved")
+                        nc.scalar.copy(half_moved[:], half_done[:])
+                        nc.gpsimd.tensor_tensor(product[:], half_moved[:], e[:, halves[0]], MULT)
+                    else:
+                        nc.vector.tensor_tensor(product[:], half_done[:], e[:, halves[0]], MULT)
+                    waiting.append((n, product))
+                if makes:
+                    if n_made < LATE:
+                        column = ahead_of[group - LEAD][:, COLUMNS, i, :]
+                    else:
+                        column = columns_late[:, :, n_made - LATE]
+                    nc.tensor.matmul(
+                        bank[:, FORMS, i, :], column, rows_flipped[:, n_made, :], start=True, stop=True
+                    )
+                if flips:
+                    nc.tensor.transpose(bank[:, COLUMNS, i, :], bw_bf[:, :, n_flipped], identity_bf[:])
+                if len(waiting) == BATCH + LAG or n == P - 1 - LAG:
+                    sum_over_k(waiting[:-LAG])
+                    waiting = waiting[-LAG:]
+            if flips or makes:
+                written = slice(COLUMNS if flips else FORMS, FORMS + 1 if makes else COLUMNS + 1)
+                ahead = aheads.tile([P, 2, GROUP, P], BF16, name="ahead")
+                nc.scalar.copy(ahead[:, written, :, :], bank[:, written, :, :])
+                ahead_of[group] = ahead
         sum_over_k(waiting)
 
         z_bf = held.tile([P, PAIRS], BF16, name="z_bf")

@@ -4,7 +4,7 @@ from concourse.masks import make_identity
 BF16, F32, U16 = mybir.dt.bfloat16, mybir.dt.float32, mybir.dt.uint16
 RELU = mybir.ActivationFunctionType.Relu
 IDENTITY = mybir.ActivationFunctionType.Identity
-MULT = mybir.AluOpType.mult
+MULT, ADD = mybir.AluOpType.mult, mybir.AluOpType.add
 
 P = 128
 GENES = 2048
@@ -16,6 +16,11 @@ BW_LOADS = P // BW_ROWS
 GROUP = 4
 GROUPS = P // GROUP
 LEAD = 2
+EARLY = 2 * LEAD * GROUP
+U_FIRST_LOAD = 6
+U_PER_LOAD = 2
+STAGING = 8
+VECTOR_ROUNDS = 4
 LATE_ROWS = 8
 LATE_LOADS = P // LATE_ROWS
 LATE = (LATE_LOADS + LEAD) * GROUP
@@ -24,6 +29,7 @@ QUADRANTS = P // QUADRANT
 BATCH = 32
 LAG = 8
 SHARE = 4
+SHARE_AFTER = 3
 
 FLOPS = (
     3 * 2 * P * P * ENTRIES
@@ -39,7 +45,8 @@ def tile_recovermodel_b_kernel(
     nc = tc.nc
     with (
         tc.tile_pool(name="held", bufs=1) as held,
-        tc.tile_pool(name="staged", bufs=BW_LOADS) as staged,
+        tc.tile_pool(name="staged", bufs=STAGING) as staged,
+        tc.tile_pool(name="early", bufs=EARLY) as early,
         tc.tile_pool(name="aheads", bufs=2 * LEAD) as aheads,
         tc.tile_pool(name="moved", bufs=3) as moved,
         tc.tile_pool(name="products", bufs=BATCH + 2 * LAG) as products,
@@ -142,22 +149,41 @@ def tile_recovermodel_b_kernel(
         def weigh_on_vector(weighted, block, weights):
             nc.vector.tensor_scalar(weighted, block, weights, None, MULT)
 
+        u_weighted = []
+
+        def make_u(n):
+            u_bank = banks.tile([P, PAIRS], F32, name="u_bank", tag="bank")
+            nc.tensor.matmul(u_bank[:], bw_bf[:, n, :], e[:, halves[0]], start=True, stop=True)
+            u_sb = early.tile([P, PAIRS], F32, name="u_sb")
+            weigh = weigh_on_scalar if n % 2 == 0 else weigh_on_vector
+            weigh(u_sb[:], u_bank[:], bd_flipped[:, n : n + 1])
+            u_weighted.append(u_sb)
+
         for load_no in range(BW_LOADS):
             rows = slice(load_no * BW_ROWS, (load_no + 1) * BW_ROWS)
-            nc.vector.tensor_copy(bw_bf[:, rows, :], bw_staged[load_no][:])
-            bank = banks.tile([P, BW_ROWS, P], BF16, name="rows_bank", tag="bank")
-            for i in range(BW_ROWS):
-                nc.tensor.transpose(bank[:, i, :], bw_bf[:, load_no * BW_ROWS + i, :], identity_bf[:])
-            weigh = weigh_on_scalar if load_no % 2 == 0 else weigh_on_vector
-            for i in range(BW_ROWS):
-                n = load_no * BW_ROWS + i
-                weigh(rows_flipped[:, n, :], bank[:, i, :], bd_flipped[:, n : n + 1])
+            if load_no % VECTOR_ROUNDS == VECTOR_ROUNDS - 1:
+                nc.vector.tensor_copy(bw_bf[:, rows, :], bw_staged[load_no][:])
+            else:
+                nc.gpsimd.tensor_scalar(bw_bf[:, rows, :], bw_staged[load_no][:], 1.0, 0.0, MULT, ADD)
+            if load_no * BW_ROWS >= EARLY:
+                bank = banks.tile([P, BW_ROWS, P], BF16, name="rows_bank", tag="bank")
+                for i in range(BW_ROWS):
+                    nc.tensor.transpose(
+                        bank[:, i, :], bw_bf[:, load_no * BW_ROWS + i, :], identity_bf[:]
+                    )
+                weigh = weigh_on_scalar if load_no % 2 == 0 else weigh_on_vector
+                for i in range(BW_ROWS):
+                    n = load_no * BW_ROWS + i
+                    weigh(rows_flipped[:, n, :], bank[:, i, :], bd_flipped[:, n : n + 1])
+            if load_no >= U_FIRST_LOAD:
+                for n in range(len(u_weighted), min(len(u_weighted) + U_PER_LOAD, EARLY)):
+                    make_u(n)
 
         columns_late = held.tile([P, P, P - LATE], BF16, name="columns_late")
 
         def round_late_columns(load_no):
             rows = slice(load_no * LATE_ROWS, (load_no + 1) * LATE_ROWS)
-            nc.scalar.copy(columns_late[:, rows, :], late_staged[load_no][:])
+            nc.gpsimd.tensor_scalar(columns_late[:, rows, :], late_staged[load_no][:], 1.0, 0.0, MULT, ADD)
 
         z = sums.tile([P, PAIRS], F32, name="z")
 
@@ -175,34 +201,30 @@ def tile_recovermodel_b_kernel(
         COLUMNS, FORMS = 0, 1
         ahead_of = {}
         waiting = []
-        for group in range(-2 * LEAD, GROUPS):
-            flips = 0 <= (group + 2 * LEAD) * GROUP < LATE
-            makes = 0 <= group + LEAD < GROUPS
+        for group in range(GROUPS):
+            flips = (group + 2 * LEAD) * GROUP < LATE
+            makes = EARLY <= (group + LEAD) * GROUP < P
             if flips or makes:
                 bank = blocks.tile([P, 2, GROUP, P], BF16, name="ahead_bank")
-            if 0 <= group < LATE_LOADS:
-                round_late_columns(group)
             for i in range(GROUP):
                 n = group * GROUP + i
                 n_made = n + LEAD * GROUP
                 n_flipped = n + 2 * LEAD * GROUP
-                if group >= 0:
-                    half_done = banks.tile([P, PAIRS], F32, name="half_done", tag="bank")
-                    nc.tensor.matmul(
-                        half_done[:],
-                        ahead_of[group - LEAD][:, FORMS, i, :],
-                        e[:, halves[1]],
-                        start=True,
-                        stop=True,
-                    )
-                    product = products.tile([P, PAIRS], BF16, name="product")
-                    if n % SHARE == 0:
-                        half_moved = moved.tile([P, PAIRS], F32, name="half_moved")
-                        nc.scalar.copy(half_moved[:], half_done[:])
-                        nc.gpsimd.tensor_tensor(product[:], half_moved[:], e[:, halves[0]], MULT)
-                    else:
-                        nc.vector.tensor_tensor(product[:], half_done[:], e[:, halves[0]], MULT)
-                    waiting.append((n, product))
+                if n < EARLY:
+                    stationary, other_factor = bw_bf[:, :, n], u_weighted[n][:]
+                else:
+                    stationary, other_factor = ahead_of[group - LEAD][:, FORMS, i, :], e[:, halves[0]]
+                half_done = banks.tile([P, PAIRS], F32, name="half_done", tag="bank")
+                nc.tensor.matmul(half_done[:], stationary, e[:, halves[1]], start=True, stop=True)
+                product = products.tile([P, PAIRS], BF16, name="product")
+                share = SHARE if group < LATE_LOADS else SHARE_AFTER
+                if n % share == 0 and group < GROUPS - 1:
+                    half_moved = moved.tile([P, PAIRS], F32, name="half_moved")
+                    nc.scalar.copy(half_moved[:], half_done[:])
+                    nc.gpsimd.tensor_tensor(product[:], half_moved[:], other_factor, MULT)
+                else:
+                    nc.vector.tensor_tensor(product[:], half_done[:], other_factor, MULT)
+                waiting.append((n, product))
                 if makes:
                     if n_made < LATE:
                         column = ahead_of[group - LEAD][:, COLUMNS, i, :]
@@ -221,6 +243,8 @@ def tile_recovermodel_b_kernel(
                 ahead = aheads.tile([P, 2, GROUP, P], BF16, name="ahead")
                 nc.scalar.copy(ahead[:, written, :, :], bank[:, written, :, :])
                 ahead_of[group] = ahead
+            if group < LATE_LOADS:
+                round_late_columns(group)
         sum_over_k(waiting)
 
         z_bf = held.tile([P, PAIRS], BF16, name="z_bf")

@@ -23,7 +23,8 @@ STAGING = 8
 VECTOR_ROUNDS = 4
 LATE_ROWS = 8
 LATE_LOADS = P // LATE_ROWS
-LATE = (LATE_LOADS + LEAD) * GROUP
+LATE_GROUPS = 12
+LATE = (LATE_GROUPS + LEAD) * GROUP
 QUADRANT = 32
 QUADRANTS = P // QUADRANT
 BATCH = 32
@@ -183,7 +184,12 @@ def tile_recovermodel_b_kernel(
 
         def round_late_columns(load_no):
             rows = slice(load_no * LATE_ROWS, (load_no + 1) * LATE_ROWS)
-            nc.gpsimd.tensor_scalar(columns_late[:, rows, :], late_staged[load_no][:], 1.0, 0.0, MULT, ADD)
+            if load_no % 2 == 0:
+                nc.gpsimd.tensor_scalar(
+                    columns_late[:, rows, :], late_staged[load_no][:], 1.0, 0.0, MULT, ADD
+                )
+            else:
+                nc.scalar.copy(columns_late[:, rows, :], late_staged[load_no][:])
 
         z = sums.tile([P, PAIRS], F32, name="z")
 
@@ -201,6 +207,7 @@ def tile_recovermodel_b_kernel(
         COLUMNS, FORMS = 0, 1
         ahead_of = {}
         waiting = []
+        late_rounded = 0
         for group in range(GROUPS):
             flips = (group + 2 * LEAD) * GROUP < LATE
             makes = EARLY <= (group + LEAD) * GROUP < P
@@ -217,7 +224,7 @@ def tile_recovermodel_b_kernel(
                 half_done = banks.tile([P, PAIRS], F32, name="half_done", tag="bank")
                 nc.tensor.matmul(half_done[:], stationary, e[:, halves[1]], start=True, stop=True)
                 product = products.tile([P, PAIRS], BF16, name="product")
-                share = SHARE if group < LATE_LOADS else SHARE_AFTER
+                share = SHARE if group < LATE_GROUPS else SHARE_AFTER
                 if n % share == 0 and group < GROUPS - 1:
                     half_moved = moved.tile([P, PAIRS], F32, name="half_moved")
                     nc.scalar.copy(half_moved[:], half_done[:])
@@ -243,14 +250,18 @@ def tile_recovermodel_b_kernel(
                 ahead = aheads.tile([P, 2, GROUP, P], BF16, name="ahead")
                 nc.scalar.copy(ahead[:, written, :, :], bank[:, written, :, :])
                 ahead_of[group] = ahead
-            if group < LATE_LOADS:
-                round_late_columns(group)
+            while late_rounded * LATE_GROUPS < (group + 1) * LATE_LOADS and late_rounded < LATE_LOADS:
+                round_late_columns(late_rounded)
+                late_rounded += 1
         sum_over_k(waiting)
 
         z_bf = held.tile([P, PAIRS], BF16, name="z_bf")
-        nc.scalar.activation(z_bf[:], z[:], IDENTITY, bias=boff_sb[:, 0:1])
-        combined = banks.tile([P, PAIRS], F32, name="combined", tag="bank")
-        nc.tensor.matmul(combined[:], wc1_sb[:], z_bf[:], start=True, stop=True)
         out_sb = held.tile([P, PAIRS], F32, name="out_sb")
-        nc.scalar.activation(out_sb[:], combined[:], RELU, bias=bc1_sb[:, 0:1])
-        nc.sync.dma_start(out, out_sb[:])
+        pieces = [slice(h * (PAIRS // 2), (h + 1) * (PAIRS // 2)) for h in range(2)]
+        for piece in pieces:
+            nc.scalar.activation(z_bf[:, piece], z[:, piece], IDENTITY, bias=boff_sb[:, 0:1])
+        for piece in pieces:
+            combined = banks.tile([P, PAIRS // 2], F32, name="combined", tag="bank")
+            nc.tensor.matmul(combined[:], wc1_sb[:], z_bf[:, piece], start=True, stop=True)
+            nc.scalar.activation(out_sb[:, piece], combined[:], RELU, bias=bc1_sb[:, 0:1])
+            nc.sync.dma_start(out[:, piece], out_sb[:, piece])

@@ -20,7 +20,7 @@ EARLY = 2 * LEAD * GROUP
 U_FIRST_LOAD = 6
 U_PER_LOAD = 2
 STAGING = 8
-VECTOR_ROUNDS = 4
+VECTOR_ROUNDS = 16
 LATE_ROWS = 8
 LATE_LOADS = P // LATE_ROWS
 LATE_GROUPS = 12

@@ -31,6 +31,7 @@ BATCH = 32
 LAG = 8
 SHARE = 4
 SHARE_AFTER = 3
+MOVED = 6
 
 FLOPS = (
     3 * 2 * P * P * ENTRIES
@@ -49,7 +50,7 @@ def tile_recovermodel_b_kernel(
         tc.tile_pool(name="staged", bufs=STAGING) as staged,
         tc.tile_pool(name="early", bufs=EARLY) as early,
         tc.tile_pool(name="aheads", bufs=2 * LEAD) as aheads,
-        tc.tile_pool(name="moved", bufs=3) as moved,
+        tc.tile_pool(name="moved", bufs=MOVED) as moved,
         tc.tile_pool(name="products", bufs=BATCH + 2 * LAG) as products,
         tc.psum_pool(name="sums", bufs=1) as sums,
         tc.psum_pool(name="blocks", bufs=2) as blocks,

@@ -143,7 +143,7 @@ def tile_recovermodel_b_kernel(
         nc.vector.tensor_copy(bd_flipped[:], bd_bank[:])
 
         bw_bf = held.tile([P, P, P], BF16, name="bw_bf")
-        rows_flipped = held.tile([P, P, P], BF16, name="rows_flipped")
+        rows_flipped = held.tile([P, P - EARLY, P], BF16, name="rows_flipped")
 
         def weigh_on_scalar(weighted, block, weights):
             nc.scalar.activation(weighted, block, IDENTITY, scale=weights)
@@ -176,7 +176,7 @@ def tile_recovermodel_b_kernel(
                 weigh = weigh_on_scalar if load_no % 2 == 0 else weigh_on_vector
                 for i in range(BW_ROWS):
                     n = load_no * BW_ROWS + i
-                    weigh(rows_flipped[:, n, :], bank[:, i, :], bd_flipped[:, n : n + 1])
+                    weigh(rows_flipped[:, n - EARLY, :], bank[:, i, :], bd_flipped[:, n : n + 1])
             if load_no >= U_FIRST_LOAD:
                 for n in range(len(u_weighted), min(len(u_weighted) + U_PER_LOAD, EARLY)):
                     make_u(n)
@@ -239,7 +239,7 @@ def tile_recovermodel_b_kernel(
                     else:
                         column = columns_late[:, :, n_made - LATE]
                     nc.tensor.matmul(
-                        bank[:, FORMS, i, :], column, rows_flipped[:, n_made, :], start=True, stop=True
+                        bank[:, FORMS, i, :], column, rows_flipped[:, n_made - EARLY, :], start=True, stop=True
                     )
                 if flips:
                     nc.tensor.transpose(bank[:, COLUMNS, i, :], bw_bf[:, :, n_flipped], identity_bf[:])

import concourse.mybir as mybir
from concourse.masks import make_identity

BF16, F32, U16 = mybir.dt.bfloat16, mybir.dt.float32, mybir.dt.uint16
RELU = mybir.ActivationFunctionType.Relu
IDENTITY = mybir.ActivationFunctionType.Identity
MULT, ADD = mybir.AluOpType.mult, mybir.AluOpType.add

P = 128
GENES = 2048
PAIRS = 512
ENTRIES = 2 * PAIRS
GENE_BLOCKS = GENES // P
BW_ROWS = 8
BW_LOADS = P // BW_ROWS
GROUP = 4
GROUPS = P // GROUP
LEAD = 2
EARLY = 2 * LEAD * GROUP
U_FIRST_LOAD = 6
U_PER_LOAD = 2
STAGING = 8
VECTOR_ROUNDS = 16
LATE_ROWS = 8
LATE_LOADS = P // LATE_ROWS
LATE_GROUPS = 12
LATE = (LATE_GROUPS + LEAD) * GROUP
QUADRANT = 32
QUADRANTS = P // QUADRANT
BATCH = 32
LAG = 8
SHARE = 4
SHARE_AFTER = 3
MOVED = 6

FLOPS = (
    3 * 2 * P * P * ENTRIES
    + 2 * 2 * P * P * P * PAIRS
    + 3 * P * P * PAIRS
    + 2 * P * P * PAIRS
)


def tile_recovermodel_b_kernel(
    tc, table, w1, b1, w2, b2, w3, b3, bw, bd, boff, wc1, bc1, offs, out
):
    nc = tc.nc
    with (
        tc.tile_pool(name="held", bufs=1) as held,
        tc.tile_pool(name="staged", bufs=STAGING) as staged,
        tc.tile_pool(name="early", bufs=EARLY) as early,
        tc.tile_pool(name="aheads", bufs=2 * LEAD) as aheads,
        tc.tile_pool(name="moved", bufs=MOVED) as moved,
        tc.tile_pool(name="products", bufs=BATCH + 2 * LAG) as products,
        tc.psum_pool(name="sums", bufs=1) as sums,
        tc.psum_pool(name="blocks", bufs=2) as blocks,
        tc.psum_pool(name="banks", bufs=5) as banks,
    ):
        offsets = held.tile([P, ENTRIES // 16], U16, name="offsets")
        nc.sync.dma_start(offsets[:], offs)

        genes = held.tile([P, GENE_BLOCKS, P], BF16, name="genes")
        nc.sync.dma_start(genes[:], table.rearrange("(a p) k -> p a k", p=P))

        def load(queue, source, shape, dtype, name):
            loaded = held.tile(shape, dtype, name=name)
            queue.dma_start(loaded[:], source)
            return loaded

        bd_sb = load(nc.sync, bd, [P, P], F32, "bd_sb")

        w1_sb = load(nc.scalar, w1, [P, P], BF16, "w1_sb")
        b1_sb = load(nc.scalar, b1, [P, 1], F32, "b1_sb")
        w2_sb = load(nc.scalar, w2, [P, P], BF16, "w2_sb")
        b2_sb = load(nc.scalar, b2, [P, 1], F32, "b2_sb")
        w3_sb = load(nc.scalar, w3, [P, P], BF16, "w3_sb")
        b3_sb = load(nc.scalar, b3, [P, 1], F32, "b3_sb")

        bw_staged = []
        for load_no in range(BW_LOADS):
            bw_f32 = staged.tile([P, BW_ROWS, P], F32, name="bw_f32", tag="bw_f32")
            nc.sync.dma_start(bw_f32[:], bw[:, load_no * BW_ROWS : (load_no + 1) * BW_ROWS, :])
            bw_staged.append(bw_f32)

        late_staged = []
        for load_no in range(LATE_LOADS):
            rows = slice(load_no * LATE_ROWS, (load_no + 1) * LATE_ROWS)
            late_f32 = staged.tile([P, LATE_ROWS, P - LATE], F32, name="late_f32", tag="bw_f32")
            nc.sync.dma_start(late_f32[:], bw[rows, :, LATE:].rearrange("j m n -> m j n"))
            late_staged.append(late_f32)

        bc1_sb = load(nc.sync, bc1, [P, 1], F32, "bc1_sb")
        wc1_sb = held.tile([P, P], BF16, name="wc1_sb")
        boff_sb = held.tile([P, 1], F32, name="boff_sb")
        for q in range(QUADRANTS):
            rows = slice(q * QUADRANT, (q + 1) * QUADRANT)
            nc.sync.dma_start(wc1_sb[rows, :], wc1.rearrange("(r q) c -> q r c", q=QUADRANTS)[q])
            nc.sync.dma_start(boff_sb[rows, :], boff.rearrange("(r q) o -> q r o", q=QUADRANTS)[q])

        identity_bf = held.tile([P, P], BF16, name="identity_bf")
        make_identity(nc, identity_bf[:])
        identity_f32 = held.tile([P, P], F32, name="identity_f32")
        make_identity(nc, identity_f32[:])

        pick = held.tile([P, QUADRANT, QUADRANT], BF16, name="pick")
        nc.gpsimd.memset(pick[:], 0.0)
        nc.gpsimd.memset(pick[:].rearrange("k r c -> k (r c)")[:, :: QUADRANT + 1], 1.0)

        window = held.tile([P, GENES], BF16, name="window")
        for group in range(GENE_BLOCKS // 4):
            flipped = banks.tile([P, 4 * P], BF16, name="flipped", tag="bank")
            for a in range(4):
                nc.tensor.transpose(
                    flipped[:, a * P : (a + 1) * P], genes[:, 4 * group + a, :], identity_bf[:]
                )
            nc.vector.tensor_copy(window[:, group * 4 * P : (group + 1) * 4 * P], flipped[:])

        halves = [slice(h * PAIRS, (h + 1) * PAIRS) for h in range(2)]
        h1 = held.tile([P, ENTRIES], BF16, name="h1")
        h2 = held.tile([P, ENTRIES], BF16, name="h2")
        e = held.tile([P, ENTRIES], BF16, name="e")

        looked_up = []
        for h in range(2):
            layer1 = banks.tile([P, PAIRS], F32, name="layer1", tag="bank")
            piece = offsets[:, h * (PAIRS // 16) : (h + 1) * (PAIRS // 16)]
            nc.tensor.matmul(layer1[:], w1_sb[:], window[:].indirect(piece), start=True, stop=True)
            looked_up.append(layer1)
        for h in range(2):
            nc.scalar.activation(h1[:, halves[h]], looked_up[h][:], RELU, bias=b1_sb[:, 0:1])
        for h in range(2):
            layer2 = banks.tile([P, PAIRS], F32, name="layer2", tag="bank")
            nc.tensor.matmul(layer2[:], w2_sb[:], h1[:, halves[h]], start=True, stop=True)
            nc.scalar.activation(h2[:, halves[h]], layer2[:], RELU, bias=b2_sb[:, 0:1])
        for h in range(2):
            layer3 = banks.tile([P, PAIRS], F32, name="layer3", tag="bank")
            nc.tensor.matmul(layer3[:], w3_sb[:], h2[:, halves[h]], start=True, stop=True)
            nc.scalar.activation(e[:, halves[h]], layer3[:], IDENTITY, bias=b3_sb[:, 0:1])

        bd_bank = banks.tile([P, P], F32, name="bd_bank", tag="bank")
        nc.tensor.transpose(bd_bank[:], bd_sb[:], identity_f32[:])
        bd_flipped = held.tile([P, P], F32, name="bd_flipped")
        nc.vector.tensor_copy(bd_flipped[:], bd_bank[:])

        bw_bf = held.tile([P, P, P], BF16, name="bw_bf")
        rows_flipped = held.tile([P, P - EARLY, P], BF16, name="rows_flipped")

        def weigh_on_scalar(weighted, block, weights):
            nc.scalar.activation(weighted, block, IDENTITY, scale=weights)

        def weigh_on_vector(weighted, block, weights):
            nc.vector.tensor_scalar(weighted, block, weights, None, MULT)

        u_weighted = []

        def make_u(n):
            u_bank = banks.tile([P, PAIRS], F32, name="u_bank", tag="bank")
            nc.tensor.matmul(u_bank[:], bw_bf[:, n, :], e[:, halves[0]], start=True, stop=True)
            u_sb = early.tile([P, PAIRS], F32, name="u_sb")
            weigh = weigh_on_scalar if n % 2 == 0 else weigh_on_vector
            weigh(u_sb[:], u_bank[:], bd_flipped[:, n : n + 1])
            u_weighted.append(u_sb)

        for load_no in range(BW_LOADS):
            rows = slice(load_no * BW_ROWS, (load_no + 1) * BW_ROWS)
            if load_no % VECTOR_ROUNDS == VECTOR_ROUNDS - 1:
                nc.vector.tensor_copy(bw_bf[:, rows, :], bw_staged[load_no][:])
            else:
                nc.gpsimd.tensor_scalar(bw_bf[:, rows, :], bw_staged[load_no][:], 1.0, 0.0, MULT, ADD)
            if load_no * BW_ROWS >= EARLY:
                bank = banks.tile([P, BW_ROWS, P], BF16, name="rows_bank", tag="bank")
                for i in range(BW_ROWS):
                    nc.tensor.transpose(
                        bank[:, i, :], bw_bf[:, load_no * BW_ROWS + i, :], identity_bf[:]
                    )
                weigh = weigh_on_scalar if load_no % 2 == 0 else weigh_on_vector
                for i in range(BW_ROWS):
                    n = load_no * BW_ROWS + i
                    weigh(rows_flipped[:, n - EARLY, :], bank[:, i, :], bd_flipped[:, n : n + 1])
            if load_no >= U_FIRST_LOAD:
                for n in range(len(u_weighted), min(len(u_weighted) + U_PER_LOAD, EARLY)):
                    make_u(n)

        columns_late = held.tile([P, P, P - LATE], BF16, name="columns_late")

        def round_late_columns(load_no):
            rows = slice(load_no * LATE_ROWS, (load_no + 1) * LATE_ROWS)
            if load_no % 2 == 0:
                nc.gpsimd.tensor_scalar(
                    columns_late[:, rows, :], late_staged[load_no][:], 1.0, 0.0, MULT, ADD
                )
            else:
                nc.scalar.copy(columns_late[:, rows, :], late_staged[load_no][:])

        z = sums.tile([P, PAIRS], F32, name="z")

        def sum_over_k(batch):
            for n, product in batch:
                q, r = n % QUADRANTS, n // QUADRANTS
                nc.tensor.matmul(
                    z[q * QUADRANT : (q + 1) * QUADRANT, :],
                    pick[:, r, :],
                    product[:],
                    start=(r == 0),
                    stop=(r == QUADRANT - 1),
                )

        COLUMNS, FORMS = 0, 1
        ahead_of = {}
        waiting = []
        late_rounded = 0
        for group in range(GROUPS):
            flips = (group + 2 * LEAD) * GROUP < LATE
            makes = EARLY <= (group + LEAD) * GROUP < P
            if flips or makes:
                bank = blocks.tile([P, 2, GROUP, P], BF16, name="ahead_bank")
            for i in range(GROUP):
                n = group * GROUP + i
                n_made = n + LEAD * GROUP
                n_flipped = n + 2 * LEAD * GROUP
                if n < EARLY:
                    stationary, other_factor = bw_bf[:, :, n], u_weighted[n][:]
                else:
                    stationary, other_factor = ahead_of[group - LEAD][:, FORMS, i, :], e[:, halves[0]]
                half_done = banks.tile([P, PAIRS], F32, name="half_done", tag="bank")
                nc.tensor.matmul(half_done[:], stationary, e[:, halves[1]], start=True, stop=True)
                product = products.tile([P, PAIRS], BF16, name="product")
                share = SHARE if group < LATE_GROUPS else SHARE_AFTER
                if n % share == 0 and group < GROUPS - 1:
                    half_moved = moved.tile([P, PAIRS], F32, name="half_moved")
                    nc.scalar.copy(half_moved[:], half_done[:])
                    nc.gpsimd.tensor_tensor(product[:], half_moved[:], other_factor, MULT)
                else:
                    nc.vector.tensor_tensor(product[:], half_done[:], other_factor, MULT)
                waiting.append((n, product))
                if makes:
                    if n_made < LATE:
                        column = ahead_of[group - LEAD][:, COLUMNS, i, :]
                    else:
                        column = columns_late[:, :, n_made - LATE]
                    nc.tensor.matmul(
                        bank[:, FORMS, i, :], column, rows_flipped[:, n_made - EARLY, :], start=True, stop=True
                    )
                if flips:
                    nc.tensor.transpose(bank[:, COLUMNS, i, :], bw_bf[:, :, n_flipped], identity_bf[:])
                if len(waiting) == BATCH + LAG or n == P - 1 - LAG:
                    sum_over_k(waiting[:-LAG])
                    waiting = waiting[-LAG:]
            if flips or makes:
                written = slice(COLUMNS if flips else FORMS, FORMS + 1 if makes else COLUMNS + 1)
                ahead = aheads.tile([P, 2, GROUP, P], BF16, name="ahead")
                nc.scalar.copy(ahead[:, written, :, :], bank[:, written, :, :])
                ahead_of[group] = ahead
            while late_rounded * LATE_GROUPS < (group + 1) * LATE_LOADS and late_rounded < LATE_LOADS:
                round_late_columns(late_rounded)
                late_rounded += 1
        sum_over_k(waiting)

        z_bf = held.tile([P, PAIRS], BF16, name="z_bf")
        out_sb = held.tile([P, PAIRS], F32, name="out_sb")
        pieces = [slice(h * (PAIRS // 2), (h + 1) * (PAIRS // 2)) for h in range(2)]
        for piece in pieces:
            nc.scalar.activation(z_bf[:, piece], z[:, piece], IDENTITY, bias=boff_sb[:, 0:1])
        for piece in pieces:
            combined = banks.tile([P, PAIRS // 2], F32, name="combined", tag="bank")
            nc.tensor.matmul(combined[:], wc1_sb[:], z_bf[:, piece], start=True, stop=True)
            nc.scalar.activation(out_sb[:, piece], combined[:], RELU, bias=bc1_sb[:, 0:1])
            nc.sync.dma_start(out[:, piece], out_sb[:, piece])
